import numpy as np
import ml_dtypes


def mxq(x, axis, fmt="e4m3"):
    dtype, down = {"e4m3": (ml_dtypes.float8_e4m3fn, 7), "e5m2": (ml_dtypes.float8_e5m2, 14)}[fmt]
    v = np.moveaxis(np.asarray(x, np.float32).astype(ml_dtypes.bfloat16).astype(np.float64), axis, -1)
    blocks = v.reshape(v.shape[:-1] + (-1, 32))
    amax = np.abs(blocks).max(-1, keepdims=True)
    byte = np.maximum(np.where(amax > 0, np.frexp(amax)[1] - 1 + 127, 0) - down, 1)
    scale = np.exp2(byte - 127.0)
    codes = (blocks / scale).astype(np.float32).astype(dtype).astype(np.float64)
    return np.moveaxis((codes * scale).reshape(v.shape), -1, axis)


WIDE = False


def mx_kscale(k):
    if not WIDE:
        return np.ones(k)
    levels = np.array([20, -20, 10, -10, 0])
    a = np.random.permutation(np.resize(levels, k // 512 * 4)).reshape(k // 512, 4)
    idx = np.arange(k)
    return np.exp2(a[idx // 512, idx % 128 // 32])


BF16 = ml_dtypes.bfloat16


def bf(x):
    return np.asarray(x, np.float32).astype(BF16)


def f64(x):
    return np.asarray(x).astype(np.float64)


B, T, C, H, NOPE, ROPE, VD, LORA = 1, 512, 2048, 16, 128, 128, 128, 512
QK = NOPE + ROPE
HALF = ROPE // 2


def make_freq_cis():
    inv = 1.0 / (10000.0 ** (np.arange(0, ROPE, 2) / ROPE))
    ang = np.outer(np.arange(T), inv)
    return np.stack([np.cos(ang), np.sin(ang)], -1)


def apply_rope(v, fc):
    vr = v.reshape(B, T, H, HALF, 2)
    f = fc.reshape(1, T, 1, HALF, 2)
    real = vr[..., 0] * f[..., 0] - vr[..., 1] * f[..., 1]
    imag = vr[..., 1] * f[..., 0] + vr[..., 0] * f[..., 1]
    return np.stack([real, imag], -1).reshape(B, T, H, ROPE)


def apply_rope_adjoint(g, fc):
    gr = g.reshape(B, T, H, HALF, 2)
    f = fc.reshape(1, T, 1, HALF, 2)
    a = gr[..., 0] * f[..., 0] + gr[..., 1] * f[..., 1]
    b = gr[..., 1] * f[..., 0] - gr[..., 0] * f[..., 1]
    return np.stack([a, b], -1).reshape(B, T, H, ROPE)


def setup_inputs():
    u = mx_kscale(H * QK)
    u = np.repeat(u[::2], 2)
    x = np.random.standard_normal((B, T, C))
    fc = make_freq_cis()
    Wq = np.random.standard_normal((C, H * QK)) * 2.0 / np.sqrt(C) / u[None, :]
    g = np.random.standard_normal((B, T, H, QK)) * np.exp2(np.random.randint(-12, 1, (B, T, 1, 1))) * 8.0 * u.reshape(H, QK)
    return {"x": bf(x), "freq_cis": bf(fc), "Wq": bf(Wq), "grad_out": bf(g)}


def reference(x, freq_cis, Wq, grad_out):
    g = f64(grad_out)
    gp = np.concatenate([g[..., :NOPE], apply_rope_adjoint(g[..., NOPE:], f64(freq_cis))], -1).reshape(B, T, H * QK)
    return mxq(gp, 2, "e5m2") @ mxq(f64(Wq), 1, "e4m3").T

@@ -1,0 +1,178 @@
+from contextlib import ExitStack
+
+import concourse.mybir as mybir
+from concourse.masks import make_identity
+
+BF16 = mybir.dt.bfloat16
+F32 = mybir.dt.float32
+U32 = mybir.dt.uint32
+U8 = mybir.dt.uint8
+E4M3X4 = mybir.dt.float8_e4m3fn_x4
+E5M2X4 = mybir.dt.float8_e5m2_x4
+MULT = mybir.AluOpType.mult
+ADD = mybir.AluOpType.add
+
+P = 128
+TOKENS = 512
+COLUMNS = 2048
+HEADS = 16
+HEAD = 256
+KEPT = 128
+PAIRS = (HEAD - KEPT) // 2
+K = HEADS * HEAD
+PACK = 4
+PASSES = K // (P * PACK)
+BLOCKS = K // 2 // P
+BANK_BLOCKS = 4
+N = 512
+WAVES = TOKENS // P
+TILES_PER_WAVE = N // P
+HALF_HEADS = HEADS // 2
+WEIGHT_BUFS = 6
+GRAD_BUFS = 2
+
+FLOPS = 2 * TOKENS * K * COLUMNS
+BYTES = 2 * (TOKENS * 2 * PAIRS + COLUMNS * K + TOKENS * K) + 4 * TOKENS * COLUMNS
+
+
+def new_products(wave):
+    if wave < 0:
+        return []
+    return [(wave, n) for n in range(wave)] + [(m, wave) for m in range(wave + 1)]
+
+
+def tile_multiheadlatentattention_pb_kernel(tc, x, freq_cis, Wq, grad_out, out):
+    nc = tc.nc
+    grad_rows = grad_out[0].rearrange("(m p) h f -> m p (h f)", p=P)
+    weight_rows = Wq.rearrange("(c p) k -> c p k", p=P)
+    out_rows = out[0].rearrange("(m p) c -> m p c", p=P)
+
+    with ExitStack() as ctx:
+        keep = ctx.enter_context(tc.tile_pool(name="keep", bufs=1))
+        grads = ctx.enter_context(tc.tile_pool(name="grads", bufs=GRAD_BUFS))
+        weights = ctx.enter_context(tc.tile_pool(name="weights", bufs=WEIGHT_BUFS))
+        products = ctx.enter_context(tc.tile_pool(name="products", bufs=1))
+        staging = ctx.enter_context(tc.tile_pool(name="staging", bufs=4))
+        results = ctx.enter_context(tc.tile_pool(name="results", bufs=4))
+        banks = ctx.enter_context(tc.psum_pool(name="banks", bufs=6))
+        sums = ctx.enter_context(tc.psum_pool(name="sums", bufs=2))
+        ctx.enter_context(tc.manual_schedule())
+
+        grad_codes = keep.tile([P, WAVES, PASSES * P], U32, align_bytes=64)
+        grad_scales = keep.tile([P, WAVES, PASSES * P], U8, align_bytes=64)
+        weight_codes = keep.tile([P, WAVES, PASSES, N], U32, align_bytes=64)
+        weight_scales = keep.tile([P, WAVES, PASSES, N], U8, align_bytes=64)
+
+        identity = keep.tile([P, P], F32)
+        make_identity(nc, identity[:])
+
+        table = keep.tile([P, WAVES, 2 * PAIRS], BF16)
+        nc.scalar.dma_start(out=table[:], in_=freq_cis.rearrange("(m p) i two -> p m (i two)", p=P))
+        cos_sin = table[:].rearrange("p m (i two) -> p m i two", two=2)
+        minus_sin = keep.tile([P, WAVES, PAIRS], BF16)
+        nc.vector.tensor_scalar_mul(out=minus_sin[:], in0=cos_sin[:, :, :, 1], scalar1=-1.0)
+
+        grad_tiles = {}
+        weight_tiles = {}
+
+        def load_grad(m):
+            grad = grads.tile([P, K], BF16, name="grad")
+            for half in range(2):
+                cols = slice(half * K // 2, (half + 1) * K // 2)
+                nc.sync.dma_start(out=grad[:, cols], in_=grad_rows[m][:, cols])
+            grad_tiles[m] = grad
+
+        def load_weight(c):
+            weight = weights.tile([P, K], BF16, name="weight")
+            nc.sync.dma_start(out=weight[:], in_=weight_rows[c])
+            weight_tiles[c] = weight
+
+        def rotate(m):
+            heads = grad_tiles[m][:].rearrange("p (h f) -> p h f", f=HEAD)
+            for half in range(2):
+                some = slice(half * HALF_HEADS, (half + 1) * HALF_HEADS)
+                pairs = heads[:, some, KEPT:HEAD].rearrange("p h (i e) -> p h i e", e=2)
+                cos = cos_sin[:, m, :, 0:1].unsqueeze(1).to_broadcast([P, HALF_HEADS, PAIRS, 2])
+                sin = cos_sin[:, m, :, 1].unsqueeze(1).to_broadcast([P, HALF_HEADS, PAIRS])
+                neg = minus_sin[:, m, :].unsqueeze(1).to_broadcast([P, HALF_HEADS, PAIRS])
+                by_cos = products.tile([P, HALF_HEADS, PAIRS, 2], F32)
+                nc.vector.tensor_tensor(out=by_cos[:], in0=pairs, in1=cos, op=MULT)
+                by_sin = products.tile([P, HALF_HEADS, 2, PAIRS], F32)
+                nc.vector.tensor_tensor(out=by_sin[:, :, 0, :], in0=pairs[:, :, :, 1], in1=sin, op=MULT)
+                nc.vector.tensor_tensor(out=by_sin[:, :, 1, :], in0=pairs[:, :, :, 0], in1=neg, op=MULT)
+                nc.vector.tensor_tensor(
+                    out=pairs, in0=by_cos[:], in1=by_sin[:].rearrange("p h e i -> p h i e"), op=ADD
+                )
+
+        def transpose(rows):
+            words = rows[:].bitcast(F32)
+            staged = staging.tile([P, K], BF16, align_bytes=64)
+            staged_words = staged[:].bitcast(F32).rearrange("p (g r u) -> p g r u", r=P, u=2)
+            for first in range(0, BLOCKS, BANK_BLOCKS):
+                bank = banks.tile([P, BANK_BLOCKS, P], F32)
+                for b in range(BANK_BLOCKS):
+                    block = slice((first + b) * P, (first + b + 1) * P)
+                    nc.tensor.transpose(bank[:, b, :], words[:, block], identity[:])
+                nc.scalar.copy(
+                    out=staged_words[:, first // 2 : first // 2 + 2, :, :],
+                    in_=bank[:].rearrange("p (g u) r -> p g r u", u=2),
+                )
+            return staged
+
+        def prepare_grad(m):
+            staged = transpose(grad_tiles[m])
+            if m + GRAD_BUFS < WAVES:
+                load_grad(m + GRAD_BUFS)
+            nc.vector.quantize_mx(
+                out=grad_codes[:, m, :].bitcast(E5M2X4), scales=grad_scales[:, m, :], in_=staged[:]
+            )
+
+        def prepare_weight(c):
+            staged = transpose(weight_tiles[c])
+            if c + WEIGHT_BUFS < WAVES * TILES_PER_WAVE:
+                load_weight(c + WEIGHT_BUFS)
+            n = c // TILES_PER_WAVE
+            cols = slice(c % TILES_PER_WAVE * P, (c % TILES_PER_WAVE + 1) * P)
+            for g in range(PASSES):
+                nc.vector.quantize_mx(
+                    out=weight_codes[:, n, g, cols].bitcast(E4M3X4),
+                    scales=weight_scales[:, n, g, cols],
+                    in_=staged[:, g * P * PACK : (g + 1) * P * PACK],
+                )
+
+        def multiply(m, n):
+            total = sums.tile([P, N], F32)
+            for g in range(PASSES):
+                tokens = slice(g * P, (g + 1) * P)
+                nc.tensor.matmul_mx(
+                    out=total[:],
+                    lhsT=grad_codes[:, m, tokens].bitcast(E5M2X4),
+                    lhsT_scale=grad_scales[:, m, tokens],
+                    rhs=weight_codes[:, n, g, :].bitcast(E4M3X4),
+                    rhs_scale=weight_scales[:, n, g, :],
+                    start=(g == 0),
+                    stop=(g == PASSES - 1),
+                )
+            result = results.tile([P, N], F32)
+            nc.scalar.copy(out=result[:], in_=total[:])
+            nc.sync.dma_start(out=out_rows[m][:, n * N : (n + 1) * N], in_=result[:])
+
+        load_grad(0)
+        for c in range(TILES_PER_WAVE):
+            load_weight(c)
+        load_grad(1)
+        for c in range(TILES_PER_WAVE, WEIGHT_BUFS):
+            load_weight(c)
+
+        for wave in range(WAVES):
+            rotate(wave)
+            ready = new_products(wave - 1)
+            for step in range(TILES_PER_WAVE + 1):
+                if step == TILES_PER_WAVE - 1:
+                    prepare_grad(wave)
+                else:
+                    prepare_weight(wave * TILES_PER_WAVE + min(step, TILES_PER_WAVE - 1))
+                if step < len(ready):
+                    multiply(*ready[step])
+        for m, n in new_products(WAVES - 1):
+            multiply(m, n)

@@ -51,7 +51,7 @@ def tile_multiheadlatentattention_pb_kernel(tc, x, freq_cis, Wq, grad_out, out):
         keep = ctx.enter_context(tc.tile_pool(name="keep", bufs=1))
         grads = ctx.enter_context(tc.tile_pool(name="grads", bufs=GRAD_BUFS))
         weights = ctx.enter_context(tc.tile_pool(name="weights", bufs=WEIGHT_BUFS))
-        products = ctx.enter_context(tc.tile_pool(name="products", bufs=1))
+        products = ctx.enter_context(tc.tile_pool(name="products", bufs=2))
         staging = ctx.enter_context(tc.tile_pool(name="staging", bufs=4))
         results = ctx.enter_context(tc.tile_pool(name="results", bufs=4))
         banks = ctx.enter_context(tc.psum_pool(name="banks", bufs=6))
@@ -66,21 +66,25 @@ def tile_multiheadlatentattention_pb_kernel(tc, x, freq_cis, Wq, grad_out, out):
         identity = keep.tile([P, P], F32)
         make_identity(nc, identity[:])
 
-        table = keep.tile([P, WAVES, 2 * PAIRS], BF16)
-        nc.scalar.dma_start(out=table[:], in_=freq_cis.rearrange("(m p) i two -> p m (i two)", p=P))
-        cos_sin = table[:].rearrange("p m (i two) -> p m i two", two=2)
-        minus_sin = keep.tile([P, WAVES, PAIRS], BF16)
-        nc.vector.tensor_scalar_mul(out=minus_sin[:], in0=cos_sin[:, :, :, 1], scalar1=-1.0)
+        turn = keep.tile([P, WAVES, 2, PAIRS, 2], BF16)
+        nc.scalar.dma_start(
+            out=turn[:, :, 0, :, :], in_=freq_cis.rearrange("(m p) i two -> p m i two", p=P)
+        )
+        nc.vector.tensor_scalar_mul(out=turn[:, :, 1, :, 0], in0=turn[:, :, 0, :, 1], scalar1=-1.0)
+        nc.vector.tensor_copy(out=turn[:, :, 1, :, 1], in_=turn[:, :, 0, :, 0])
 
         grad_tiles = {}
         weight_tiles = {}
 
+        def load_grad_half(m, half):
+            if half == 0:
+                grad_tiles[m] = grads.tile([P, K], BF16, name="grad")
+            cols = slice(half * K // 2, (half + 1) * K // 2)
+            nc.sync.dma_start(out=grad_tiles[m][:, cols], in_=grad_rows[m][:, cols])
+
         def load_grad(m):
-            grad = grads.tile([P, K], BF16, name="grad")
-            for half in range(2):
-                cols = slice(half * K // 2, (half + 1) * K // 2)
-                nc.sync.dma_start(out=grad[:, cols], in_=grad_rows[m][:, cols])
-            grad_tiles[m] = grad
+            load_grad_half(m, 0)
+            load_grad_half(m, 1)
 
         def load_weight(c):
             weight = weights.tile([P, K], BF16, name="weight")
@@ -89,19 +93,26 @@ def tile_multiheadlatentattention_pb_kernel(tc, x, freq_cis, Wq, grad_out, out):
 
         def rotate(m):
             heads = grad_tiles[m][:].rearrange("p (h f) -> p h f", f=HEAD)
-            for half in range(2):
-                some = slice(half * HALF_HEADS, (half + 1) * HALF_HEADS)
-                pairs = heads[:, some, KEPT:HEAD].rearrange("p h (i e) -> p h i e", e=2)
-                cos = cos_sin[:, m, :, 0:1].unsqueeze(1).to_broadcast([P, HALF_HEADS, PAIRS, 2])
-                sin = cos_sin[:, m, :, 1].unsqueeze(1).to_broadcast([P, HALF_HEADS, PAIRS])
-                neg = minus_sin[:, m, :].unsqueeze(1).to_broadcast([P, HALF_HEADS, PAIRS])
-                by_cos = products.tile([P, HALF_HEADS, PAIRS, 2], F32)
-                nc.vector.tensor_tensor(out=by_cos[:], in0=pairs, in1=cos, op=MULT)
-                by_sin = products.tile([P, HALF_HEADS, 2, PAIRS], F32)
-                nc.vector.tensor_tensor(out=by_sin[:, :, 0, :], in0=pairs[:, :, :, 1], in1=sin, op=MULT)
-                nc.vector.tensor_tensor(out=by_sin[:, :, 1, :], in0=pairs[:, :, :, 0], in1=neg, op=MULT)
+            factors = turn[:, m].rearrange("p j i e -> p j (i e)").unsqueeze(1)
+            shape = [P, HALF_HEADS, 2, 2 * PAIRS]
+            halves = [slice(half * HALF_HEADS, (half + 1) * HALF_HEADS) for half in range(2)]
+            terms = []
+            for some in halves:
+                term = products.tile(shape, F32, name="term")
                 nc.vector.tensor_tensor(
-                    out=pairs, in0=by_cos[:], in1=by_sin[:].rearrange("p h e i -> p h i e"), op=ADD
+                    out=term[:],
+                    in0=heads[:, some, KEPT:HEAD].unsqueeze(2).to_broadcast(shape),
+                    in1=factors.to_broadcast(shape),
+                    op=MULT,
+                )
+                terms.append(term)
+            for some, term in zip(halves, terms):
+                pair = term[:].rearrange("p h j (i e) -> p h i j e", e=2)
+                nc.vector.tensor_tensor(
+                    out=heads[:, some, KEPT:HEAD].rearrange("p h (i j) -> p h i j", j=2),
+                    in0=pair[:, :, :, :, 0],
+                    in1=pair[:, :, :, :, 1],
+                    op=ADD,
                 )
 
         def transpose(rows):
@@ -157,8 +168,10 @@ def tile_multiheadlatentattention_pb_kernel(tc, x, freq_cis, Wq, grad_out, out):
             nc.scalar.copy(out=result[:], in_=total[:])
             nc.sync.dma_start(out=out_rows[m][:, n * N : (n + 1) * N], in_=result[:])
 
-        load_grad(0)
-        for c in range(TILES_PER_WAVE):
+        load_grad_half(0, 0)
+        load_weight(0)
+        load_grad_half(0, 1)
+        for c in range(1, TILES_PER_WAVE):
             load_weight(c)
         load_grad(1)
         for c in range(TILES_PER_WAVE, WEIGHT_BUFS):

@@ -30,6 +30,7 @@ TILES_PER_WAVE = N // P
 HALF_HEADS = HEADS // 2
 WEIGHT_BUFS = 6
 GRAD_BUFS = 2
+IDLE_MATMULS = 2
 
 FLOPS = 2 * TOKENS * K * COLUMNS
 BYTES = 2 * (TOKENS * 2 * PAIRS + COLUMNS * K + TOKENS * K) + 4 * TOKENS * COLUMNS
@@ -72,6 +73,14 @@ def tile_multiheadlatentattention_pb_kernel(tc, x, freq_cis, Wq, grad_out, out):
         )
         nc.vector.tensor_scalar_mul(out=turn[:, :, 1, :, 0], in0=turn[:, :, 0, :, 1], scalar1=-1.0)
         nc.vector.tensor_copy(out=turn[:, :, 1, :, 1], in_=turn[:, :, 0, :, 0])
+
+        zeros = keep.tile([P, N], BF16)
+        nc.vector.memset(zeros[:], 0.0)
+
+        def hold_clock():
+            unread = sums.tile([P, N], F32, name="total")
+            for i in range(IDLE_MATMULS):
+                nc.tensor.matmul(out=unread[:], lhsT=zeros[:, 0:P], rhs=zeros[:], start=True, stop=True)
 
         grad_tiles = {}
         weight_tiles = {}
@@ -152,7 +161,7 @@ def tile_multiheadlatentattention_pb_kernel(tc, x, freq_cis, Wq, grad_out, out):
                 )
 
         def multiply(m, n):
-            total = sums.tile([P, N], F32)
+            total = sums.tile([P, N], F32, name="total")
             for g in range(PASSES):
                 tokens = slice(g * P, (g + 1) * P)
                 nc.tensor.matmul_mx(
@@ -187,5 +196,7 @@ def tile_multiheadlatentattention_pb_kernel(tc, x, freq_cis, Wq, grad_out, out):
                     prepare_weight(wave * TILES_PER_WAVE + min(step, TILES_PER_WAVE - 1))
                 if step < len(ready):
                     multiply(*ready[step])
+                else:
+                    hold_clock()
         for m, n in new_products(WAVES - 1):
             multiply(m, n)

@@ -22,47 +22,53 @@ PAIRS = (HEAD - KEPT) // 2
 K = HEADS * HEAD
 PACK = 4
 PASSES = K // (P * PACK)
-BLOCKS = K // 2 // P
-BANK_BLOCKS = 4
 N = 512
 WAVES = TOKENS // P
-TILES_PER_WAVE = N // P
-HALF_HEADS = HEADS // 2
-WEIGHT_BUFS = 6
-GRAD_BUFS = 2
+ROW_TILES = N // P
+SLICES = 4
+SLICE = K // SLICES
+SLICE_HEADS = HEADS // SLICES
+SLICE_PASSES = PASSES // SLICES
+SLICE_BLOCKS = SLICE // 2 // P
+STEPS = WAVES * SLICES
+SUM_BANKS = 4
+WEIGHT_AHEAD = 3
+GRAD_AHEAD = 4
 IDLE_MATMULS = 2
 
 FLOPS = 2 * TOKENS * K * COLUMNS
 BYTES = 2 * (TOKENS * 2 * PAIRS + COLUMNS * K + TOKENS * K) + 4 * TOKENS * COLUMNS
 
 
-def new_products(wave):
-    if wave < 0:
-        return []
-    return [(wave, n) for n in range(wave)] + [(m, wave) for m in range(wave + 1)]
+def products_in_order():
+    order = []
+    for wave in range(WAVES):
+        order.extend([(m, wave) for m in range(wave + 1)])
+        order.extend([(wave, n) for n in range(wave)])
+    return order
 
 
 def tile_multiheadlatentattention_pb_kernel(tc, x, freq_cis, Wq, grad_out, out):
     nc = tc.nc
     grad_rows = grad_out[0].rearrange("(m p) h f -> m p (h f)", p=P)
-    weight_rows = Wq.rearrange("(c p) k -> c p k", p=P)
+    weight_rows = Wq.rearrange("(n j p) k -> n p j k", j=ROW_TILES, p=P)
     out_rows = out[0].rearrange("(m p) c -> m p c", p=P)
 
     with ExitStack() as ctx:
         keep = ctx.enter_context(tc.tile_pool(name="keep", bufs=1))
-        grads = ctx.enter_context(tc.tile_pool(name="grads", bufs=GRAD_BUFS))
-        weights = ctx.enter_context(tc.tile_pool(name="weights", bufs=WEIGHT_BUFS))
+        grads = ctx.enter_context(tc.tile_pool(name="grads", bufs=GRAD_AHEAD + 2))
+        weights = ctx.enter_context(tc.tile_pool(name="weights", bufs=WEIGHT_AHEAD + 1))
         products = ctx.enter_context(tc.tile_pool(name="products", bufs=2))
-        staging = ctx.enter_context(tc.tile_pool(name="staging", bufs=4))
+        staging = ctx.enter_context(tc.tile_pool(name="staging", bufs=3))
         results = ctx.enter_context(tc.tile_pool(name="results", bufs=4))
-        banks = ctx.enter_context(tc.psum_pool(name="banks", bufs=6))
-        sums = ctx.enter_context(tc.psum_pool(name="sums", bufs=2))
+        banks = ctx.enter_context(tc.psum_pool(name="banks", bufs=8 - SUM_BANKS))
+        sums = ctx.enter_context(tc.psum_pool(name="sums", bufs=1))
         ctx.enter_context(tc.manual_schedule())
 
         grad_codes = keep.tile([P, WAVES, PASSES * P], U32, align_bytes=64)
         grad_scales = keep.tile([P, WAVES, PASSES * P], U8, align_bytes=64)
-        weight_codes = keep.tile([P, WAVES, PASSES, N], U32, align_bytes=64)
-        weight_scales = keep.tile([P, WAVES, PASSES, N], U8, align_bytes=64)
+        weight_codes = keep.tile([P, WAVES, PASSES * N], U32, align_bytes=64)
+        weight_scales = keep.tile([P, WAVES, PASSES * N], U8, align_bytes=64)
 
         identity = keep.tile([P, P], F32)
         make_identity(nc, identity[:])
@@ -77,126 +83,168 @@ def tile_multiheadlatentattention_pb_kernel(tc, x, freq_cis, Wq, grad_out, out):
         zeros = keep.tile([P, N], BF16)
         nc.vector.memset(zeros[:], 0.0)
 
-        def hold_clock():
-            unread = sums.tile([P, N], F32, name="total")
-            for i in range(IDLE_MATMULS):
-                nc.tensor.matmul(out=unread[:], lhsT=zeros[:, 0:P], rhs=zeros[:], start=True, stop=True)
-
         grad_tiles = {}
         weight_tiles = {}
+        term_tiles = {}
+        staged_tiles = {}
 
-        def load_grad_half(m, half):
-            if half == 0:
-                grad_tiles[m] = grads.tile([P, K], BF16, name="grad")
-            cols = slice(half * K // 2, (half + 1) * K // 2)
-            nc.sync.dma_start(out=grad_tiles[m][:, cols], in_=grad_rows[m][:, cols])
+        def place(step):
+            return step // SLICES, step % SLICES
 
-        def load_grad(m):
-            load_grad_half(m, 0)
-            load_grad_half(m, 1)
+        def load_grad(step):
+            if step >= STEPS:
+                return
+            m, s = place(step)
+            grad = grads.tile([P, SLICE], BF16, name="grad")
+            nc.sync.dma_start(out=grad[:], in_=grad_rows[m][:, s * SLICE : (s + 1) * SLICE])
+            grad_tiles[step] = grad
 
-        def load_weight(c):
-            weight = weights.tile([P, K], BF16, name="weight")
-            nc.sync.dma_start(out=weight[:], in_=weight_rows[c])
-            weight_tiles[c] = weight
+        def load_weight(step, pieces):
+            if step >= STEPS:
+                return
+            n, s = place(step)
+            weight = weights.tile([P, ROW_TILES, SLICE], BF16, name="weight")
+            share = ROW_TILES // pieces
+            for piece in range(pieces):
+                rows = slice(piece * share, (piece + 1) * share)
+                nc.sync.dma_start(
+                    out=weight[:, rows, :], in_=weight_rows[n][:, rows, s * SLICE : (s + 1) * SLICE]
+                )
+            weight_tiles[step] = weight
 
-        def rotate(m):
-            heads = grad_tiles[m][:].rearrange("p (h f) -> p h f", f=HEAD)
+        def rotate_products(step):
+            if step >= STEPS:
+                return
+            m, s = place(step)
+            heads = grad_tiles[step][:].rearrange("p (h f) -> p h f", f=HEAD)
             factors = turn[:, m].rearrange("p j i e -> p j (i e)").unsqueeze(1)
-            shape = [P, HALF_HEADS, 2, 2 * PAIRS]
-            halves = [slice(half * HALF_HEADS, (half + 1) * HALF_HEADS) for half in range(2)]
-            terms = []
-            for some in halves:
-                term = products.tile(shape, F32, name="term")
-                nc.vector.tensor_tensor(
-                    out=term[:],
-                    in0=heads[:, some, KEPT:HEAD].unsqueeze(2).to_broadcast(shape),
-                    in1=factors.to_broadcast(shape),
-                    op=MULT,
-                )
-                terms.append(term)
-            for some, term in zip(halves, terms):
-                pair = term[:].rearrange("p h j (i e) -> p h i j e", e=2)
-                nc.vector.tensor_tensor(
-                    out=heads[:, some, KEPT:HEAD].rearrange("p h (i j) -> p h i j", j=2),
-                    in0=pair[:, :, :, :, 0],
-                    in1=pair[:, :, :, :, 1],
-                    op=ADD,
-                )
+            shape = [P, SLICE_HEADS, 2, 2 * PAIRS]
+            term = products.tile(shape, F32, name="term")
+            nc.vector.tensor_tensor(
+                out=term[:],
+                in0=heads[:, :, KEPT:HEAD].unsqueeze(2).to_broadcast(shape),
+                in1=factors.to_broadcast(shape),
+                op=MULT,
+            )
+            term_tiles[step] = term
 
-        def transpose(rows):
-            words = rows[:].bitcast(F32)
-            staged = staging.tile([P, K], BF16, align_bytes=64)
-            staged_words = staged[:].bitcast(F32).rearrange("p (g r u) -> p g r u", r=P, u=2)
-            for first in range(0, BLOCKS, BANK_BLOCKS):
-                bank = banks.tile([P, BANK_BLOCKS, P], F32)
-                for b in range(BANK_BLOCKS):
-                    block = slice((first + b) * P, (first + b + 1) * P)
-                    nc.tensor.transpose(bank[:, b, :], words[:, block], identity[:])
-                nc.scalar.copy(
-                    out=staged_words[:, first // 2 : first // 2 + 2, :, :],
-                    in_=bank[:].rearrange("p (g u) r -> p g r u", u=2),
-                )
-            return staged
-
-        def prepare_grad(m):
-            staged = transpose(grad_tiles[m])
-            if m + GRAD_BUFS < WAVES:
-                load_grad(m + GRAD_BUFS)
-            nc.vector.quantize_mx(
-                out=grad_codes[:, m, :].bitcast(E5M2X4), scales=grad_scales[:, m, :], in_=staged[:]
+        def rotate_sums(step):
+            if step >= STEPS:
+                return
+            heads = grad_tiles[step][:].rearrange("p (h f) -> p h f", f=HEAD)
+            pair = term_tiles[step][:].rearrange("p h j (i e) -> p h i j e", e=2)
+            nc.vector.tensor_tensor(
+                out=heads[:, :, KEPT:HEAD].rearrange("p h (i j) -> p h i j", j=2),
+                in0=pair[:, :, :, :, 0],
+                in1=pair[:, :, :, :, 1],
+                op=ADD,
             )
 
-        def prepare_weight(c):
-            staged = transpose(weight_tiles[c])
-            if c + WEIGHT_BUFS < WAVES * TILES_PER_WAVE:
-                load_weight(c + WEIGHT_BUFS)
-            n = c // TILES_PER_WAVE
-            cols = slice(c % TILES_PER_WAVE * P, (c % TILES_PER_WAVE + 1) * P)
-            for g in range(PASSES):
-                nc.vector.quantize_mx(
-                    out=weight_codes[:, n, g, cols].bitcast(E4M3X4),
-                    scales=weight_scales[:, n, g, cols],
-                    in_=staged[:, g * P * PACK : (g + 1) * P * PACK],
-                )
+        def transpose_rows(words, staged_words):
+            bank = banks.tile([P, SLICE_BLOCKS, P], F32, name="bank")
+            for b in range(SLICE_BLOCKS):
+                nc.tensor.transpose(bank[:, b, :], words[:, b * P : (b + 1) * P], identity[:])
+            nc.scalar.copy(out=staged_words, in_=bank[:].rearrange("p (g u) r -> p g r u", u=2))
 
-        def multiply(m, n):
-            total = sums.tile([P, N], F32, name="total")
-            for g in range(PASSES):
-                tokens = slice(g * P, (g + 1) * P)
+        def transpose(step):
+            staged_weight = staging.tile([P, ROW_TILES * SLICE], BF16, align_bytes=64, name="staged_weight")
+            staged_grad = staging.tile([P, SLICE], BF16, align_bytes=64, name="staged_grad")
+            weight_words = staged_weight[:].bitcast(F32).rearrange("p (g r u) -> p g r u", g=SLICE_PASSES, u=2)
+            grad_words = staged_grad[:].bitcast(F32).rearrange("p (g r u) -> p g r u", g=SLICE_PASSES, u=2)
+            for j in range(ROW_TILES):
+                transpose_rows(
+                    weight_tiles[step][:, j, :].bitcast(F32), weight_words[:, :, j * P : (j + 1) * P, :]
+                )
+            transpose_rows(grad_tiles[step][:].bitcast(F32), grad_words)
+            staged_tiles[step] = (staged_weight, staged_grad)
+
+        def quantise_weight(step):
+            n, s = place(step)
+            cols = slice(s * SLICE_PASSES * N, (s + 1) * SLICE_PASSES * N)
+            nc.vector.quantize_mx(
+                out=weight_codes[:, n, cols].bitcast(E4M3X4),
+                scales=weight_scales[:, n, cols],
+                in_=staged_tiles[step][0][:],
+            )
+
+        def quantise_grad(step):
+            m, s = place(step)
+            cols = slice(s * SLICE_PASSES * P, (s + 1) * SLICE_PASSES * P)
+            nc.vector.quantize_mx(
+                out=grad_codes[:, m, cols].bitcast(E5M2X4),
+                scales=grad_scales[:, m, cols],
+                in_=staged_tiles[step][1][:],
+            )
+
+        waiting = products_in_order()
+        open_groups = []
+        free_banks = list(range(SUM_BANKS))
+
+        def multiply_slice(group):
+            m, n, s, total, bank = group
+            for g in range(s * SLICE_PASSES, (s + 1) * SLICE_PASSES):
                 nc.tensor.matmul_mx(
                     out=total[:],
-                    lhsT=grad_codes[:, m, tokens].bitcast(E5M2X4),
-                    lhsT_scale=grad_scales[:, m, tokens],
-                    rhs=weight_codes[:, n, g, :].bitcast(E4M3X4),
-                    rhs_scale=weight_scales[:, n, g, :],
+                    lhsT=grad_codes[:, m, g * P : (g + 1) * P].bitcast(E5M2X4),
+                    lhsT_scale=grad_scales[:, m, g * P : (g + 1) * P],
+                    rhs=weight_codes[:, n, g * N : (g + 1) * N].bitcast(E4M3X4),
+                    rhs_scale=weight_scales[:, n, g * N : (g + 1) * N],
                     start=(g == 0),
                     stop=(g == PASSES - 1),
                 )
-            result = results.tile([P, N], F32)
+            group[2] = s + 1
+
+        def store(group):
+            m, n, s, total, bank = group
+            result = results.tile([P, N], F32, name="result")
             nc.scalar.copy(out=result[:], in_=total[:])
             nc.sync.dma_start(out=out_rows[m][:, n * N : (n + 1) * N], in_=result[:])
 
-        load_grad_half(0, 0)
-        load_weight(0)
-        load_grad_half(0, 1)
-        for c in range(1, TILES_PER_WAVE):
-            load_weight(c)
-        load_grad(1)
-        for c in range(TILES_PER_WAVE, WEIGHT_BUFS):
-            load_weight(c)
+        def multiply_ready(step):
+            busy = True
+            while busy:
+                while free_banks and waiting and SLICES * max(waiting[0]) <= step:
+                    m, n = waiting[0]
+                    waiting.remove((m, n))
+                    bank = free_banks[0]
+                    free_banks.remove(bank)
+                    total = sums.tile([P, N], F32, name="total%d" % bank)
+                    open_groups.append([m, n, 0, total, bank])
+                busy = False
+                for group in list(open_groups):
+                    while group[2] < SLICES and SLICES * max(group[0], group[1]) + group[2] <= step:
+                        multiply_slice(group)
+                        busy = True
+                    if group[2] == SLICES:
+                        store(group)
+                        open_groups.remove(group)
+                        free_banks.append(group[4])
 
-        for wave in range(WAVES):
-            rotate(wave)
-            ready = new_products(wave - 1)
-            for step in range(TILES_PER_WAVE + 1):
-                if step == TILES_PER_WAVE - 1:
-                    prepare_grad(wave)
-                else:
-                    prepare_weight(wave * TILES_PER_WAVE + min(step, TILES_PER_WAVE - 1))
-                if step < len(ready):
-                    multiply(*ready[step])
-                else:
-                    hold_clock()
-        for m, n in new_products(WAVES - 1):
-            multiply(m, n)
+        def hold_clock():
+            unread = sums.tile([P, N], F32, name="total%d" % (SUM_BANKS - 1))
+            for i in range(IDLE_MATMULS):
+                nc.tensor.matmul(out=unread[:], lhsT=zeros[:, 0:P], rhs=zeros[:], start=True, stop=True)
+
+        load_grad(0)
+        load_weight(0, ROW_TILES)
+        for step in range(1, WEIGHT_AHEAD):
+            load_grad(step)
+            load_weight(step, 1)
+        for step in range(WEIGHT_AHEAD, GRAD_AHEAD):
+            load_grad(step)
+        rotate_products(0)
+        rotate_sums(0)
+        rotate_products(1)
+
+        for step in range(STEPS):
+            transpose(step)
+            load_weight(step + WEIGHT_AHEAD, 1)
+            load_grad(step + GRAD_AHEAD)
+            rotate_sums(step + 1)
+            quantise_weight(step)
+            rotate_products(step + 2)
+            quantise_grad(step)
+            multiply_ready(step - 1)
+            if step < SLICES:
+                hold_clock()
+        multiply_ready(STEPS - 1)

@@ -31,7 +31,8 @@ SLICE_HEADS = HEADS // SLICES
 SLICE_PASSES = PASSES // SLICES
 SLICE_BLOCKS = SLICE // 2 // P
 STEPS = WAVES * SLICES
-SUM_BANKS = 4
+SUM_BANKS = 3
+MULTIPLY_BEHIND = 2
 WEIGHT_AHEAD = 3
 GRAD_AHEAD = 4
 IDLE_MATMULS = 2
@@ -244,7 +245,7 @@ def tile_multiheadlatentattention_pb_kernel(tc, x, freq_cis, Wq, grad_out, out):
             quantise_weight(step)
             rotate_products(step + 2)
             quantise_grad(step)
-            multiply_ready(step - 1)
+            multiply_ready(step - MULTIPLY_BEHIND)
             if step < SLICES:
                 hold_clock()
         multiply_ready(STEPS - 1)

@@ -33,6 +33,7 @@ SLICE_BLOCKS = SLICE // 2 // P
 STEPS = WAVES * SLICES
 SUM_BANKS = 3
 MULTIPLY_BEHIND = 2
+STEP_PASSES = 6
 WEIGHT_AHEAD = 3
 GRAD_AHEAD = 4
 IDLE_MATMULS = 2
@@ -78,11 +79,13 @@ def tile_multiheadlatentattention_pb_kernel(tc, x, freq_cis, Wq, grad_out, out):
         nc.scalar.dma_start(
             out=turn[:, :, 0, :, :], in_=freq_cis.rearrange("(m p) i two -> p m i two", p=P)
         )
-        nc.vector.tensor_scalar_mul(out=turn[:, :, 1, :, 0], in0=turn[:, :, 0, :, 1], scalar1=-1.0)
-        nc.vector.tensor_copy(out=turn[:, :, 1, :, 1], in_=turn[:, :, 0, :, 0])
+        nc.vector.tensor_scalar_mul(out=turn[:, 0, 1, :, 0], in0=turn[:, 0, 0, :, 1], scalar1=-1.0)
+        nc.vector.tensor_copy(out=turn[:, 0, 1, :, 1], in_=turn[:, 0, 0, :, 0])
+        nc.scalar.mul(out=turn[:, 1:WAVES, 1, :, 0], in_=turn[:, 1:WAVES, 0, :, 1], mul=-1.0)
+        nc.scalar.copy(out=turn[:, 1:WAVES, 1, :, 1], in_=turn[:, 1:WAVES, 0, :, 0])
 
         zeros = keep.tile([P, N], BF16)
-        nc.vector.memset(zeros[:], 0.0)
+        nc.gpsimd.memset(zeros[:], 0.0)
 
         grad_tiles = {}
         weight_tiles = {}
@@ -201,7 +204,8 @@ def tile_multiheadlatentattention_pb_kernel(tc, x, freq_cis, Wq, grad_out, out):
             nc.scalar.copy(out=result[:], in_=total[:])
             nc.sync.dma_start(out=out_rows[m][:, n * N : (n + 1) * N], in_=result[:])
 
-        def multiply_ready(step):
+        def multiply_ready(step, limit):
+            done = 0
             busy = True
             while busy:
                 while free_banks and waiting and SLICES * max(waiting[0]) <= step:
@@ -213,8 +217,9 @@ def tile_multiheadlatentattention_pb_kernel(tc, x, freq_cis, Wq, grad_out, out):
                     open_groups.append([m, n, 0, total, bank])
                 busy = False
                 for group in list(open_groups):
-                    while group[2] < SLICES and SLICES * max(group[0], group[1]) + group[2] <= step:
+                    while group[2] < SLICES and SLICES * max(group[0], group[1]) + group[2] <= step and done < limit:
                         multiply_slice(group)
+                        done += SLICE_PASSES
                         busy = True
                     if group[2] == SLICES:
                         store(group)
@@ -245,7 +250,7 @@ def tile_multiheadlatentattention_pb_kernel(tc, x, freq_cis, Wq, grad_out, out):
             quantise_weight(step)
             rotate_products(step + 2)
             quantise_grad(step)
-            multiply_ready(step - MULTIPLY_BEHIND)
+            multiply_ready(step - MULTIPLY_BEHIND, STEP_PASSES)
             if step < SLICES:
                 hold_clock()
-        multiply_ready(STEPS - 1)
+        multiply_ready(STEPS - 1, WAVES * WAVES * PASSES)

@@ -36,7 +36,6 @@ MULTIPLY_BEHIND = 2
 STEP_PASSES = 6
 WEIGHT_AHEAD = 3
 GRAD_AHEAD = 4
-IDLE_MATMULS = 2
 
 FLOPS = 2 * TOKENS * K * COLUMNS
 BYTES = 2 * (TOKENS * 2 * PAIRS + COLUMNS * K + TOKENS * K) + 4 * TOKENS * COLUMNS
@@ -83,9 +82,6 @@ def tile_multiheadlatentattention_pb_kernel(tc, x, freq_cis, Wq, grad_out, out):
         nc.vector.tensor_copy(out=turn[:, 0, 1, :, 1], in_=turn[:, 0, 0, :, 0])
         nc.scalar.mul(out=turn[:, 1:WAVES, 1, :, 0], in_=turn[:, 1:WAVES, 0, :, 1], mul=-1.0)
         nc.scalar.copy(out=turn[:, 1:WAVES, 1, :, 1], in_=turn[:, 1:WAVES, 0, :, 0])
-
-        zeros = keep.tile([P, N], BF16)
-        nc.gpsimd.memset(zeros[:], 0.0)
 
         grad_tiles = {}
         weight_tiles = {}
@@ -226,16 +222,11 @@ def tile_multiheadlatentattention_pb_kernel(tc, x, freq_cis, Wq, grad_out, out):
                         open_groups.remove(group)
                         free_banks.append(group[4])
 
-        def hold_clock():
-            unread = sums.tile([P, N], F32, name="total%d" % (SUM_BANKS - 1))
-            for i in range(IDLE_MATMULS):
-                nc.tensor.matmul(out=unread[:], lhsT=zeros[:, 0:P], rhs=zeros[:], start=True, stop=True)
-
         load_grad(0)
         load_weight(0, ROW_TILES)
         for step in range(1, WEIGHT_AHEAD):
             load_grad(step)
-            load_weight(step, 1)
+            load_weight(step, ROW_TILES)
         for step in range(WEIGHT_AHEAD, GRAD_AHEAD):
             load_grad(step)
         rotate_products(0)
@@ -251,6 +242,4 @@ def tile_multiheadlatentattention_pb_kernel(tc, x, freq_cis, Wq, grad_out, out):
             rotate_products(step + 2)
             quantise_grad(step)
             multiply_ready(step - MULTIPLY_BEHIND, STEP_PASSES)
-            if step < SLICES:
-                hold_clock()
         multiply_ready(STEPS - 1, WAVES * WAVES * PASSES)

@@ -61,7 +61,7 @@ def tile_multiheadlatentattention_pb_kernel(tc, x, freq_cis, Wq, grad_out, out):
         weights = ctx.enter_context(tc.tile_pool(name="weights", bufs=WEIGHT_AHEAD + 1))
         products = ctx.enter_context(tc.tile_pool(name="products", bufs=2))
         staging = ctx.enter_context(tc.tile_pool(name="staging", bufs=3))
-        results = ctx.enter_context(tc.tile_pool(name="results", bufs=4))
+        results = ctx.enter_context(tc.tile_pool(name="results", bufs=WAVES * WAVES))
         banks = ctx.enter_context(tc.psum_pool(name="banks", bufs=8 - SUM_BANKS))
         sums = ctx.enter_context(tc.psum_pool(name="sums", bufs=1))
         ctx.enter_context(tc.manual_schedule())
@@ -194,11 +194,20 @@ def tile_multiheadlatentattention_pb_kernel(tc, x, freq_cis, Wq, grad_out, out):
                 )
             group[2] = s + 1
 
-        def store(group):
+        held = []
+
+        def store_held():
+            for m, n, result in held:
+                nc.sync.dma_start(out=out_rows[m][:, n * N : (n + 1) * N], in_=result[:])
+            held.clear()
+
+        def store(group, loads_over):
             m, n, s, total, bank = group
             result = results.tile([P, N], F32, name="result")
             nc.scalar.copy(out=result[:], in_=total[:])
-            nc.sync.dma_start(out=out_rows[m][:, n * N : (n + 1) * N], in_=result[:])
+            held.append((m, n, result))
+            if loads_over:
+                store_held()
 
         def multiply_ready(step, limit):
             done = 0
@@ -218,7 +227,7 @@ def tile_multiheadlatentattention_pb_kernel(tc, x, freq_cis, Wq, grad_out, out):
                         done += SLICE_PASSES
                         busy = True
                     if group[2] == SLICES:
-                        store(group)
+                        store(group, step + MULTIPLY_BEHIND + WEIGHT_AHEAD >= STEPS - 1)
                         open_groups.remove(group)
                         free_banks.append(group[4])
 

from contextlib import ExitStack

import concourse.mybir as mybir
from concourse.masks import make_identity

BF16 = mybir.dt.bfloat16
F32 = mybir.dt.float32
U32 = mybir.dt.uint32
U8 = mybir.dt.uint8
E4M3X4 = mybir.dt.float8_e4m3fn_x4
E5M2X4 = mybir.dt.float8_e5m2_x4
MULT = mybir.AluOpType.mult
ADD = mybir.AluOpType.add

P = 128
TOKENS = 512
COLUMNS = 2048
HEADS = 16
HEAD = 256
KEPT = 128
PAIRS = (HEAD - KEPT) // 2
K = HEADS * HEAD
PACK = 4
PASSES = K // (P * PACK)
N = 512
WAVES = TOKENS // P
ROW_TILES = N // P
SLICES = 4
SLICE = K // SLICES
SLICE_HEADS = HEADS // SLICES
SLICE_PASSES = PASSES // SLICES
SLICE_BLOCKS = SLICE // 2 // P
STEPS = WAVES * SLICES
SUM_BANKS = 3
MULTIPLY_BEHIND = 2
STEP_PASSES = 6
WEIGHT_AHEAD = 3
GRAD_AHEAD = 4

FLOPS = 2 * TOKENS * K * COLUMNS
BYTES = 2 * (TOKENS * 2 * PAIRS + COLUMNS * K + TOKENS * K) + 4 * TOKENS * COLUMNS


def products_in_order():
    order = []
    for wave in range(WAVES):
        order.extend([(m, wave) for m in range(wave + 1)])
        order.extend([(wave, n) for n in range(wave)])
    return order


def tile_multiheadlatentattention_pb_kernel(tc, x, freq_cis, Wq, grad_out, out):
    nc = tc.nc
    grad_rows = grad_out[0].rearrange("(m p) h f -> m p (h f)", p=P)
    weight_rows = Wq.rearrange("(n j p) k -> n p j k", j=ROW_TILES, p=P)
    out_rows = out[0].rearrange("(m p) c -> m p c", p=P)

    with ExitStack() as ctx:
        keep = ctx.enter_context(tc.tile_pool(name="keep", bufs=1))
        grads = ctx.enter_context(tc.tile_pool(name="grads", bufs=GRAD_AHEAD + 2))
        weights = ctx.enter_context(tc.tile_pool(name="weights", bufs=WEIGHT_AHEAD + 1))
        products = ctx.enter_context(tc.tile_pool(name="products", bufs=2))
        staging = ctx.enter_context(tc.tile_pool(name="staging", bufs=3))
        results = ctx.enter_context(tc.tile_pool(name="results", bufs=WAVES * WAVES))
        banks = ctx.enter_context(tc.psum_pool(name="banks", bufs=8 - SUM_BANKS))
        sums = ctx.enter_context(tc.psum_pool(name="sums", bufs=1))
        ctx.enter_context(tc.manual_schedule())

        grad_codes = keep.tile([P, WAVES, PASSES * P], U32, align_bytes=64)
        grad_scales = keep.tile([P, WAVES, PASSES * P], U8, align_bytes=64)
        weight_codes = keep.tile([P, WAVES, PASSES * N], U32, align_bytes=64)
        weight_scales = keep.tile([P, WAVES, PASSES * N], U8, align_bytes=64)

        identity = keep.tile([P, P], F32)
        make_identity(nc, identity[:])

        turn = keep.tile([P, WAVES, 2, PAIRS, 2], BF16)
        nc.scalar.dma_start(
            out=turn[:, :, 0, :, :], in_=freq_cis.rearrange("(m p) i two -> p m i two", p=P)
        )
        nc.vector.tensor_scalar_mul(out=turn[:, 0, 1, :, 0], in0=turn[:, 0, 0, :, 1], scalar1=-1.0)
        nc.vector.tensor_copy(out=turn[:, 0, 1, :, 1], in_=turn[:, 0, 0, :, 0])
        nc.scalar.mul(out=turn[:, 1:WAVES, 1, :, 0], in_=turn[:, 1:WAVES, 0, :, 1], mul=-1.0)
        nc.scalar.copy(out=turn[:, 1:WAVES, 1, :, 1], in_=turn[:, 1:WAVES, 0, :, 0])

        grad_tiles = {}
        weight_tiles = {}
        term_tiles = {}
        staged_tiles = {}

        def place(step):
            return step // SLICES, step % SLICES

        def load_grad(step):
            if step >= STEPS:
                return
            m, s = place(step)
            grad = grads.tile([P, SLICE], BF16, name="grad")
            nc.sync.dma_start(out=grad[:], in_=grad_rows[m][:, s * SLICE : (s + 1) * SLICE])
            grad_tiles[step] = grad

        def load_weight(step, pieces):
            if step >= STEPS:
                return
            n, s = place(step)
            weight = weights.tile([P, ROW_TILES, SLICE], BF16, name="weight")
            share = ROW_TILES // pieces
            for piece in range(pieces):
                rows = slice(piece * share, (piece + 1) * share)
                nc.sync.dma_start(
                    out=weight[:, rows, :], in_=weight_rows[n][:, rows, s * SLICE : (s + 1) * SLICE]
                )
            weight_tiles[step] = weight

        def rotate_products(step):
            if step >= STEPS:
                return
            m, s = place(step)
            heads = grad_tiles[step][:].rearrange("p (h f) -> p h f", f=HEAD)
            factors = turn[:, m].rearrange("p j i e -> p j (i e)").unsqueeze(1)
            shape = [P, SLICE_HEADS, 2, 2 * PAIRS]
            term = products.tile(shape, F32, name="term")
            nc.vector.tensor_tensor(
                out=term[:],
                in0=heads[:, :, KEPT:HEAD].unsqueeze(2).to_broadcast(shape),
                in1=factors.to_broadcast(shape),
                op=MULT,
            )
            term_tiles[step] = term

        def rotate_sums(step):
            if step >= STEPS:
                return
            heads = grad_tiles[step][:].rearrange("p (h f) -> p h f", f=HEAD)
            pair = term_tiles[step][:].rearrange("p h j (i e) -> p h i j e", e=2)
            nc.vector.tensor_tensor(
                out=heads[:, :, KEPT:HEAD].rearrange("p h (i j) -> p h i j", j=2),
                in0=pair[:, :, :, :, 0],
                in1=pair[:, :, :, :, 1],
                op=ADD,
            )

        def transpose_rows(words, staged_words):
            bank = banks.tile([P, SLICE_BLOCKS, P], F32, name="bank")
            for b in range(SLICE_BLOCKS):
                nc.tensor.transpose(bank[:, b, :], words[:, b * P : (b + 1) * P], identity[:])
            nc.scalar.copy(out=staged_words, in_=bank[:].rearrange("p (g u) r -> p g r u", u=2))

        def transpose(step):
            staged_weight = staging.tile([P, ROW_TILES * SLICE], BF16, align_bytes=64, name="staged_weight")
            staged_grad = staging.tile([P, SLICE], BF16, align_bytes=64, name="staged_grad")
            weight_words = staged_weight[:].bitcast(F32).rearrange("p (g r u) -> p g r u", g=SLICE_PASSES, u=2)
            grad_words = staged_grad[:].bitcast(F32).rearrange("p (g r u) -> p g r u", g=SLICE_PASSES, u=2)
            for j in range(ROW_TILES):
                transpose_rows(
                    weight_tiles[step][:, j, :].bitcast(F32), weight_words[:, :, j * P : (j + 1) * P, :]
                )
            transpose_rows(grad_tiles[step][:].bitcast(F32), grad_words)
            staged_tiles[step] = (staged_weight, staged_grad)

        def quantise_weight(step):
            n, s = place(step)
            cols = slice(s * SLICE_PASSES * N, (s + 1) * SLICE_PASSES * N)
            nc.vector.quantize_mx(
                out=weight_codes[:, n, cols].bitcast(E4M3X4),
                scales=weight_scales[:, n, cols],
                in_=staged_tiles[step][0][:],
            )

        def quantise_grad(step):
            m, s = place(step)
            cols = slice(s * SLICE_PASSES * P, (s + 1) * SLICE_PASSES * P)
            nc.vector.quantize_mx(
                out=grad_codes[:, m, cols].bitcast(E5M2X4),
                scales=grad_scales[:, m, cols],
                in_=staged_tiles[step][1][:],
            )

        waiting = products_in_order()
        open_groups = []
        free_banks = list(range(SUM_BANKS))

        def multiply_slice(group):
            m, n, s, total, bank = group
            for g in range(s * SLICE_PASSES, (s + 1) * SLICE_PASSES):
                nc.tensor.matmul_mx(
                    out=total[:],
                    lhsT=grad_codes[:, m, g * P : (g + 1) * P].bitcast(E5M2X4),
                    lhsT_scale=grad_scales[:, m, g * P : (g + 1) * P],
                    rhs=weight_codes[:, n, g * N : (g + 1) * N].bitcast(E4M3X4),
                    rhs_scale=weight_scales[:, n, g * N : (g + 1) * N],
                    start=(g == 0),
                    stop=(g == PASSES - 1),
                )
            group[2] = s + 1

        held = []

        def store_held():
            for m, n, result in held:
                nc.sync.dma_start(out=out_rows[m][:, n * N : (n + 1) * N], in_=result[:])
            held.clear()

        def store(group, loads_over):
            m, n, s, total, bank = group
            result = results.tile([P, N], F32, name="result")
            nc.scalar.copy(out=result[:], in_=total[:])
            held.append((m, n, result))
            if loads_over:
                store_held()

        def multiply_ready(step, limit):
            done = 0
            busy = True
            while busy:
                while free_banks and waiting and SLICES * max(waiting[0]) <= step:
                    m, n = waiting[0]
                    waiting.remove((m, n))
                    bank = free_banks[0]
                    free_banks.remove(bank)
                    total = sums.tile([P, N], F32, name="total%d" % bank)
                    open_groups.append([m, n, 0, total, bank])
                busy = False
                for group in list(open_groups):
                    while group[2] < SLICES and SLICES * max(group[0], group[1]) + group[2] <= step and done < limit:
                        multiply_slice(group)
                        done += SLICE_PASSES
                        busy = True
                    if group[2] == SLICES:
                        store(group, step + MULTIPLY_BEHIND + WEIGHT_AHEAD >= STEPS - 1)
                        open_groups.remove(group)
                        free_banks.append(group[4])

        load_grad(0)
        load_weight(0, ROW_TILES)
        for step in range(1, WEIGHT_AHEAD):
            load_grad(step)
            load_weight(step, ROW_TILES)
        for step in range(WEIGHT_AHEAD, GRAD_AHEAD):
            load_grad(step)
        rotate_products(0)
        rotate_sums(0)
        rotate_products(1)

        for step in range(STEPS):
            transpose(step)
            load_weight(step + WEIGHT_AHEAD, 1)
            load_grad(step + GRAD_AHEAD)
            rotate_sums(step + 1)
            quantise_weight(step)
            rotate_products(step + 2)
            quantise_grad(step)
            multiply_ready(step - MULTIPLY_BEHIND, STEP_PASSES)
        multiply_ready(STEPS - 1, WAVES * WAVES * PASSES)
